import numpy as np
import ml_dtypes

BF16 = ml_dtypes.bfloat16


def bf(x):
    return np.asarray(x, np.float32).astype(BF16)


def f32(x):
    return np.asarray(x, np.float32)


def f64(x):
    return np.asarray(x).astype(np.float64)


def striped(idx):
    return np.tile(idx.reshape(-1, 16).T, (8, 1))


H, D, S, N, LQ, C, HD = 2, 128, 4096, 2048, 2048, 512, 256
QS = 2.0


def setup_inputs():
    return {
        "kv": f32(np.random.standard_normal((C, S))),
        "scale": f32(np.random.uniform(0.5, 1.5, (C, N))),
        "q": bf(QS * np.random.standard_normal((HD, LQ))),
        "offs": striped(np.random.permutation(S)[:N]),
    }


def reference(kv, scale, q, offs):
    idx = offs[:16].T.reshape(-1)
    kd = f64(kv)[:, idx] * f64(scale)
    qq = f64(q)
    keep = np.arange(N)[None, :] <= np.arange(LQ)[:, None]
    res = np.zeros((HD, LQ))
    for h in range(H):
        k = kd[h * D:(h + 1) * D]
        v = kd[HD + h * D:HD + (h + 1) * D]
        s = (qq[h * D:(h + 1) * D].T @ k) / np.sqrt(D)
        s = np.where(keep, s, -np.inf)
        e = np.exp(s - s.max(axis=1, keepdims=True))
        p = e / e.sum(axis=1, keepdims=True)
        res[h * D:(h + 1) * D] = v @ p.T
    return res

@@ -1,0 +1,163 @@
+import math
+
+import concourse.mybir as mybir
+from concourse.masks import make_identity
+
+F32 = mybir.dt.float32
+BF16 = mybir.dt.bfloat16
+U16 = mybir.dt.uint16
+MULT = mybir.AluOpType.mult
+POW = mybir.AluOpType.pow
+IS_GE = mybir.AluOpType.is_ge
+EXP = mybir.ActivationFunctionType.Exp
+X = mybir.AxisListType.X
+
+P = 128
+HEADS = 2
+SLOTS = 4096
+TOKENS = 2048
+PIECE = 512
+PIECES = TOKENS // PIECE
+BLOCKS = TOKENS // P
+PER = PIECE // P
+VROW = 144
+SLACK = 1.02
+
+FLOPS = HEADS * 2 * 2 * P * (TOKENS * (TOKENS + 1) // 2)
+BYTES = 4 * P * TOKENS * 4 * 2 + HEADS * P * TOKENS * (2 + 4) + TOKENS * 2
+
+
+def tile_pagedattention_b_kernel(tc, kv, scale, q, offs, out):
+    nc = tc.nc
+    with (
+        tc.tile_pool(name="held", bufs=1) as held,
+        tc.tile_pool(name="work", bufs=3) as work,
+        tc.tile_pool(name="small", bufs=4) as small,
+        tc.tile_pool(name="weights", bufs=12) as weights,
+        tc.psum_pool(name="scores", bufs=3) as scores,
+        tc.psum_pool(name="sums", bufs=1) as sums,
+        tc.psum_pool(name="spare", bufs=1) as spare,
+    ):
+        offsets = held.tile([P, TOKENS // 16], U16, name="offsets")
+        nc.sync.dma_start(offsets[:], offs)
+
+        ident_bf = held.tile([P, P], BF16, name="ident_bf")
+        make_identity(nc, ident_bf[:])
+        ident_f = held.tile([P, P], F32, name="ident_f")
+        make_identity(nc, ident_f[:])
+        ones = held.tile([P, P], BF16, name="ones")
+        nc.gpsimd.memset(ones[:], 1.0)
+        half = held.tile([P, 1], F32, name="half")
+        nc.gpsimd.memset(half[:], 0.5)
+
+        def load_channels(row, name):
+            window = held.tile([P, SLOTS], F32, name="window_" + name)
+            factors = [held.tile([P, PIECE], F32, name="factors_%s%d" % (name, p)) for p in range(PIECES)]
+            nc.sync.dma_start(factors[0][:], scale[row : row + P, 0:PIECE])
+            nc.sync.dma_start(window[:], kv[row : row + P, :])
+            for p in range(1, PIECES):
+                nc.sync.dma_start(factors[p][:], scale[row : row + P, p * PIECE : (p + 1) * PIECE])
+            return window, factors
+
+        def dequantise(channels, p, rounded):
+            window, factors = channels
+            wide = PIECE // 16
+            product = work.tile([P, PIECE], F32, name="product")
+            nc.vector.tensor_tensor(
+                product[:], window[:].indirect(offsets[:, p * wide : (p + 1) * wide]), factors[p][:], MULT
+            )
+            nc.vector.tensor_copy(rounded, product[:])
+
+        def largest_square_norm(columns, result):
+            squares = work.tile([P, PIECE], BF16, name="squares")
+            nc.vector.tensor_tensor(squares[:], columns, columns, MULT)
+            norms = spare.tile([P, PIECE], F32, name="norms", tag="spare")
+            nc.tensor.matmul(norms[:], lhsT=ones[:], rhs=squares[:], start=True, stop=True)
+            nc.vector.reduce_max(result, norms[:], axis=X)
+
+        queries, keys, values_t, shift = [], [], [], []
+        loaded = []
+        for h in range(HEADS):
+            queries.append(held.tile([P, TOKENS], BF16, name="queries%d" % h))
+            nc.sync.dma_start(queries[h][:], q[h * P : (h + 1) * P, :])
+            loaded.append((load_channels(h * P, "k%d" % h), load_channels((HEADS + h) * P, "v%d" % h)))
+
+        for h in range(HEADS):
+            k_channels, v_channels = loaded[h]
+            keys.append(held.tile([P, TOKENS], BF16, name="keys%d" % h))
+            values_t.append(held.tile([P, BLOCKS, VROW], BF16, name="values_t%d" % h))
+            shift.append(held.tile([P, PIECES], F32, name="shift%d" % h))
+            q_norm = held.tile([P, PIECES], F32, name="q_norm%d" % h)
+            k_norm = held.tile([P, PIECES], F32, name="k_norm%d" % h)
+            nc.gpsimd.memset(values_t[h][:, :, P : P + 1], 1.0)
+
+            for p in range(PIECES):
+                largest_square_norm(queries[h][:, p * PIECE : (p + 1) * PIECE], q_norm[:, p : p + 1])
+
+            for p in range(PIECES):
+                piece = keys[h][:, p * PIECE : (p + 1) * PIECE]
+                dequantise(k_channels, p, piece)
+                largest_square_norm(piece, k_norm[:, p : p + 1])
+
+                seen = small.tile([P, 1], F32, name="seen")
+                nc.vector.reduce_max(seen[:], k_norm[:, 0 : p + 1], axis=X)
+                bound_sq = small.tile([P, 1], F32, name="bound_sq")
+                nc.vector.tensor_scalar(bound_sq[:], seen[:], q_norm[:, p : p + 1], SLACK / P, op0=MULT, op1=MULT)
+                bound = small.tile([P, 1], F32, name="bound")
+                nc.gpsimd.tensor_tensor(bound[:], bound_sq[:], half[:], POW)
+                nc.gpsimd.tensor_scalar(shift[h][:, p : p + 1], bound[:], -1.0, None, op0=MULT)
+
+                values = work.tile([P, PIECE], BF16, name="values")
+                dequantise(v_channels, p, values[:])
+                flipped = spare.tile([P, PER, P], BF16, name="flipped", tag="spare")
+                for k in range(PER):
+                    nc.tensor.transpose(flipped[:, k, :], values[:, k * P : (k + 1) * P], ident_bf[:])
+                nc.vector.tensor_copy(values_t[h][:, p * PER : (p + 1) * PER, 0:P], flipped[:])
+
+        for h in range(HEADS):
+            for c in range(PIECES):
+                out_t = [sums.tile([P, P + 1], F32, name="out_t%d" % r) for r in range(PER)]
+                for jb in range(PER * (c + 1)):
+                    first = max(jb - PER * c, 0)
+                    lo = first * P
+                    st = scores.tile([P, PIECE], F32, name="st")
+                    nc.tensor.matmul(
+                        st[:, lo:],
+                        lhsT=keys[h][:, jb * P : (jb + 1) * P],
+                        rhs=queries[h][:, c * PIECE + lo : (c + 1) * PIECE],
+                        start=True,
+                        stop=True,
+                    )
+                    e = weights.tile([P, PIECE], BF16, name="e")
+                    nc.scalar.activation(
+                        e[:, lo:], st[:, lo:], EXP, bias=shift[h][:, c : c + 1], scale=1.0 / math.sqrt(P)
+                    )
+                    if jb >= PER * c:
+                        nc.gpsimd.affine_select(
+                            out=e[:, lo : lo + P],
+                            in_=e[:, lo : lo + P],
+                            pattern=[[1, P]],
+                            compare_op=IS_GE,
+                            fill=0.0,
+                            base=0,
+                            channel_multiplier=-1,
+                        )
+                    for r in range(first, PER):
+                        nc.tensor.matmul(
+                            out_t[r][:],
+                            lhsT=e[:, r * P : (r + 1) * P],
+                            rhs=values_t[h][:, jb, 0 : P + 1],
+                            start=(jb == 0),
+                            stop=(jb == PER * c + r),
+                        )
+
+                turned = spare.tile([P, PIECE], F32, name="turned", tag="spare")
+                for r in range(PER):
+                    inverse = small.tile([P, 1], F32, name="inverse")
+                    nc.vector.reciprocal(inverse[:], out_t[r][:, P : P + 1])
+                    normal = work.tile([P, P], F32, name="normal")
+                    nc.vector.tensor_scalar(normal[:], out_t[r][:, 0:P], inverse[:], None, op0=MULT)
+                    nc.tensor.transpose(turned[:, r * P : (r + 1) * P], normal[:], ident_f[:])
+                staged = work.tile([P, PIECE], F32, name="staged")
+                nc.vector.tensor_copy(staged[:], turned[:])
+                nc.sync.dma_start(out[h * P : (h + 1) * P, c * PIECE : (c + 1) * PIECE], staged[:])

@@ -31,11 +31,12 @@ def tile_pagedattention_b_kernel(tc, kv, scale, q, offs, out):
     nc = tc.nc
     with (
         tc.tile_pool(name="held", bufs=1) as held,
-        tc.tile_pool(name="work", bufs=3) as work,
+        tc.tile_pool(name="work", bufs=2) as work,
+        tc.tile_pool(name="prod", bufs=2) as prod,
         tc.tile_pool(name="small", bufs=4) as small,
-        tc.tile_pool(name="weights", bufs=12) as weights,
+        tc.tile_pool(name="weights", bufs=16) as weights,
         tc.psum_pool(name="scores", bufs=3) as scores,
-        tc.psum_pool(name="sums", bufs=1) as sums,
+        tc.psum_pool(name="sums", bufs=2) as sums,
         tc.psum_pool(name="spare", bufs=1) as spare,
     ):
         offsets = held.tile([P, TOKENS // 16], U16, name="offsets")
@@ -50,23 +51,26 @@ def tile_pagedattention_b_kernel(tc, kv, scale, q, offs, out):
         half = held.tile([P, 1], F32, name="half")
         nc.gpsimd.memset(half[:], 0.5)
 
-        def load_channels(row, name):
-            window = held.tile([P, SLOTS], F32, name="window_" + name)
-            factors = [held.tile([P, PIECE], F32, name="factors_%s%d" % (name, p)) for p in range(PIECES)]
-            nc.sync.dma_start(factors[0][:], scale[row : row + P, 0:PIECE])
-            nc.sync.dma_start(window[:], kv[row : row + P, :])
-            for p in range(1, PIECES):
-                nc.sync.dma_start(factors[p][:], scale[row : row + P, p * PIECE : (p + 1) * PIECE])
-            return window, factors
+        SLAB = SLOTS // 4
 
-        def dequantise(channels, p, rounded):
-            window, factors = channels
+        def load_window(row, name):
+            window = held.tile([P, SLOTS], F32, name="window_" + name)
+            for s in range(0, SLOTS, SLAB):
+                nc.sync.dma_start(window[:, s : s + SLAB], kv[row : row + P, s : s + SLAB])
+            return window
+
+        def load_factors(row, name, p):
+            factors = held.tile([P, PIECE], F32, name="factors_%s%d" % (name, p))
+            nc.sync.dma_start(factors[:], scale[row : row + P, p * PIECE : (p + 1) * PIECE])
+            return factors
+
+        def dequantise(window, factors, p, rounded):
             wide = PIECE // 16
-            product = work.tile([P, PIECE], F32, name="product")
+            product = prod.tile([P, PIECE], F32, name="product")
             nc.vector.tensor_tensor(
-                product[:], window[:].indirect(offsets[:, p * wide : (p + 1) * wide]), factors[p][:], MULT
+                product[:], window[:].indirect(offsets[:, p * wide : (p + 1) * wide]), factors[:], MULT
             )
-            nc.vector.tensor_copy(rounded, product[:])
+            nc.gpsimd.tensor_scalar(rounded, product[:], 1.0, None, op0=MULT)
 
         def largest_square_norm(columns, result):
             squares = work.tile([P, PIECE], BF16, name="squares")
@@ -76,88 +80,109 @@ def tile_pagedattention_b_kernel(tc, kv, scale, q, offs, out):
             nc.vector.reduce_max(result, norms[:], axis=X)
 
         queries, keys, values_t, shift = [], [], [], []
-        loaded = []
+        k_window, v_window, k_factors, v_factors = [], [], [], []
         for h in range(HEADS):
             queries.append(held.tile([P, TOKENS], BF16, name="queries%d" % h))
             nc.sync.dma_start(queries[h][:], q[h * P : (h + 1) * P, :])
-            loaded.append((load_channels(h * P, "k%d" % h), load_channels((HEADS + h) * P, "v%d" % h)))
+            k_factors.append([load_factors(h * P, "k%d" % h, 0)])
+            k_window.append(load_window(h * P, "k%d" % h))
+            v_factors.append([load_factors((HEADS + h) * P, "v%d" % h, 0)])
+            v_window.append(load_window((HEADS + h) * P, "v%d" % h))
+            for p in range(1, PIECES):
+                k_factors[h].append(load_factors(h * P, "k%d" % h, p))
+                v_factors[h].append(load_factors((HEADS + h) * P, "v%d" % h, p))
 
+        q_norm, k_norm = [], []
         for h in range(HEADS):
-            k_channels, v_channels = loaded[h]
             keys.append(held.tile([P, TOKENS], BF16, name="keys%d" % h))
             values_t.append(held.tile([P, BLOCKS, VROW], BF16, name="values_t%d" % h))
             shift.append(held.tile([P, PIECES], F32, name="shift%d" % h))
-            q_norm = held.tile([P, PIECES], F32, name="q_norm%d" % h)
-            k_norm = held.tile([P, PIECES], F32, name="k_norm%d" % h)
+            q_norm.append(held.tile([P, PIECES], F32, name="q_norm%d" % h))
+            k_norm.append(held.tile([P, PIECES], F32, name="k_norm%d" % h))
             nc.gpsimd.memset(values_t[h][:, :, P : P + 1], 1.0)
 
+        def measure_queries(h):
             for p in range(PIECES):
-                largest_square_norm(queries[h][:, p * PIECE : (p + 1) * PIECE], q_norm[:, p : p + 1])
+                largest_square_norm(queries[h][:, p * PIECE : (p + 1) * PIECE], q_norm[h][:, p : p + 1])
 
-            for p in range(PIECES):
-                piece = keys[h][:, p * PIECE : (p + 1) * PIECE]
-                dequantise(k_channels, p, piece)
-                largest_square_norm(piece, k_norm[:, p : p + 1])
+        def prepare_keys(h, p):
+            if p == 0:
+                measure_queries(h)
+            piece = keys[h][:, p * PIECE : (p + 1) * PIECE]
+            dequantise(k_window[h], k_factors[h][p], p, piece)
+            largest_square_norm(piece, k_norm[h][:, p : p + 1])
+            seen = small.tile([P, 1], F32, name="seen")
+            nc.vector.reduce_max(seen[:], k_norm[h][:, 0 : p + 1], axis=X)
+            bound_sq = small.tile([P, 1], F32, name="bound_sq")
+            nc.vector.tensor_scalar(bound_sq[:], seen[:], q_norm[h][:, p : p + 1], SLACK / P, op0=MULT, op1=MULT)
+            bound = small.tile([P, 1], F32, name="bound")
+            nc.gpsimd.tensor_tensor(bound[:], bound_sq[:], half[:], POW)
+            nc.gpsimd.tensor_scalar(shift[h][:, p : p + 1], bound[:], -1.0, None, op0=MULT)
 
-                seen = small.tile([P, 1], F32, name="seen")
-                nc.vector.reduce_max(seen[:], k_norm[:, 0 : p + 1], axis=X)
-                bound_sq = small.tile([P, 1], F32, name="bound_sq")
-                nc.vector.tensor_scalar(bound_sq[:], seen[:], q_norm[:, p : p + 1], SLACK / P, op0=MULT, op1=MULT)
-                bound = small.tile([P, 1], F32, name="bound")
-                nc.gpsimd.tensor_tensor(bound[:], bound_sq[:], half[:], POW)
-                nc.gpsimd.tensor_scalar(shift[h][:, p : p + 1], bound[:], -1.0, None, op0=MULT)
+        def prepare_values(h, p):
+            values = work.tile([P, PIECE], BF16, name="values")
+            dequantise(v_window[h], v_factors[h][p], p, values[:])
+            flipped = spare.tile([P, PER, P], BF16, name="flipped", tag="spare")
+            for k in range(PER):
+                nc.tensor.transpose(flipped[:, k, :], values[:, k * P : (k + 1) * P], ident_bf[:])
+            nc.vector.tensor_copy(values_t[h][:, p * PER : (p + 1) * PER, 0:P], flipped[:])
 
-                values = work.tile([P, PIECE], BF16, name="values")
-                dequantise(v_channels, p, values[:])
-                flipped = spare.tile([P, PER, P], BF16, name="flipped", tag="spare")
-                for k in range(PER):
-                    nc.tensor.transpose(flipped[:, k, :], values[:, k * P : (k + 1) * P], ident_bf[:])
-                nc.vector.tensor_copy(values_t[h][:, p * PER : (p + 1) * PER, 0:P], flipped[:])
-
-        for h in range(HEADS):
-            for c in range(PIECES):
-                out_t = [sums.tile([P, P + 1], F32, name="out_t%d" % r) for r in range(PER)]
-                for jb in range(PER * (c + 1)):
-                    first = max(jb - PER * c, 0)
-                    lo = first * P
-                    st = scores.tile([P, PIECE], F32, name="st")
+        chunks = [(h, c) for h in range(HEADS) for c in range(PIECES)]
+        prepare_keys(*chunks[0])
+        prepare_keys(*chunks[1])
+        prepare_values(*chunks[0])
+        for x in range(len(chunks)):
+            h, c = chunks[x]
+            out_t = [sums.tile([P, 2, P + 1], F32, name="out_t%d" % a) for a in range(PER // 2)]
+            normal = [None, None]
+            for jb in range(PER * (c + 1)):
+                first = max(jb - PER * c, 0)
+                lo = first * P
+                st = scores.tile([P, PIECE], F32, name="st")
+                nc.tensor.matmul(
+                    st[:, lo:],
+                    lhsT=keys[h][:, jb * P : (jb + 1) * P],
+                    rhs=queries[h][:, c * PIECE + lo : (c + 1) * PIECE],
+                    start=True,
+                    stop=True,
+                )
+                e = weights.tile([P, PIECE], BF16, name="e")
+                nc.scalar.activation(
+                    e[:, lo:], st[:, lo:], EXP, bias=shift[h][:, c : c + 1], scale=1.0 / math.sqrt(P)
+                )
+                if jb >= PER * c:
+                    nc.gpsimd.affine_select(
+                        out=e[:, lo : lo + P],
+                        in_=e[:, lo : lo + P],
+                        pattern=[[1, P]],
+                        compare_op=IS_GE,
+                        fill=0.0,
+                        base=0,
+                        channel_multiplier=-1,
+                    )
+                for r in range(first, PER):
                     nc.tensor.matmul(
-                        st[:, lo:],
-                        lhsT=keys[h][:, jb * P : (jb + 1) * P],
-                        rhs=queries[h][:, c * PIECE + lo : (c + 1) * PIECE],
-                        start=True,
-                        stop=True,
+                        out_t[r // 2][:, r % 2, :],
+                        lhsT=e[:, r * P : (r + 1) * P],
+                        rhs=values_t[h][:, jb, 0 : P + 1],
+                        start=(jb == 0 and r % 2 == 0),
+                        stop=(jb == PER * c + r and r % 2 == 1),
                     )
-                    e = weights.tile([P, PIECE], BF16, name="e")
-                    nc.scalar.activation(
-                        e[:, lo:], st[:, lo:], EXP, bias=shift[h][:, c : c + 1], scale=1.0 / math.sqrt(P)
-                    )
-                    if jb >= PER * c:
-                        nc.gpsimd.affine_select(
-                            out=e[:, lo : lo + P],
-                            in_=e[:, lo : lo + P],
-                            pattern=[[1, P]],
-                            compare_op=IS_GE,
-                            fill=0.0,
-                            base=0,
-                            channel_multiplier=-1,
-                        )
-                    for r in range(first, PER):
-                        nc.tensor.matmul(
-                            out_t[r][:],
-                            lhsT=e[:, r * P : (r + 1) * P],
-                            rhs=values_t[h][:, jb, 0 : P + 1],
-                            start=(jb == 0),
-                            stop=(jb == PER * c + r),
-                        )
+                if jb == 0:
+                    if x + 2 < len(chunks):
+                        prepare_keys(*chunks[x + 2])
+                    if x + 1 < len(chunks):
+                        prepare_values(*chunks[x + 1])
+                if jb >= PER * c and first % 2 == 1:
+                    a = first // 2
+                    inverse = small.tile([P, 2, 1], F32, name="inverse")
+                    nc.vector.reciprocal(inverse[:], out_t[a][:, :, P : P + 1])
+                    normal[a] = work.tile([P, 2, P], F32, name="normal")
+                    nc.vector.tensor_tensor(normal[a][:], out_t[a][:, :, 0:P], inverse[:].to_broadcast([P, 2, P]), MULT)
 
-                turned = spare.tile([P, PIECE], F32, name="turned", tag="spare")
-                for r in range(PER):
-                    inverse = small.tile([P, 1], F32, name="inverse")
-                    nc.vector.reciprocal(inverse[:], out_t[r][:, P : P + 1])
-                    normal = work.tile([P, P], F32, name="normal")
-                    nc.vector.tensor_scalar(normal[:], out_t[r][:, 0:P], inverse[:], None, op0=MULT)
-                    nc.tensor.transpose(turned[:, r * P : (r + 1) * P], normal[:], ident_f[:])
-                staged = work.tile([P, PIECE], F32, name="staged")
-                nc.vector.tensor_copy(staged[:], turned[:])
-                nc.sync.dma_start(out[h * P : (h + 1) * P, c * PIECE : (c + 1) * PIECE], staged[:])
+            turned = spare.tile([P, PIECE], F32, name="turned", tag="spare")
+            for r in range(PER):
+                nc.tensor.transpose(turned[:, r * P : (r + 1) * P], normal[r // 2][:, r % 2, :], ident_f[:])
+            staged = work.tile([P, PIECE], F32, name="staged")
+            nc.vector.tensor_copy(staged[:], turned[:])
+            nc.sync.dma_start(out[h * P : (h + 1) * P, c * PIECE : (c + 1) * PIECE], staged[:])

@@ -31,7 +31,7 @@ def tile_pagedattention_b_kernel(tc, kv, scale, q, offs, out):
     nc = tc.nc
     with (
         tc.tile_pool(name="held", bufs=1) as held,
-        tc.tile_pool(name="work", bufs=2) as work,
+        tc.tile_pool(name="work", bufs=3) as work,
         tc.tile_pool(name="prod", bufs=2) as prod,
         tc.tile_pool(name="small", bufs=4) as small,
         tc.tile_pool(name="weights", bufs=16) as weights,
@@ -48,6 +48,11 @@ def tile_pagedattention_b_kernel(tc, kv, scale, q, offs, out):
         make_identity(nc, ident_f[:])
         ones = held.tile([P, P], BF16, name="ones")
         nc.gpsimd.memset(ones[:], 1.0)
+        causal = held.tile([P, P], BF16, name="causal")
+        nc.gpsimd.memset(causal[:], 1.0)
+        nc.gpsimd.affine_select(
+            out=causal[:], in_=causal[:], pattern=[[1, P]], compare_op=IS_GE, fill=0.0, base=0, channel_multiplier=-1
+        )
         half = held.tile([P, 1], F32, name="half")
         nc.gpsimd.memset(half[:], 0.5)
 
@@ -70,7 +75,7 @@ def tile_pagedattention_b_kernel(tc, kv, scale, q, offs, out):
             nc.vector.tensor_tensor(
                 product[:], window[:].indirect(offsets[:, p * wide : (p + 1) * wide]), factors[:], MULT
             )
-            nc.gpsimd.tensor_scalar(rounded, product[:], 1.0, None, op0=MULT)
+            nc.vector.tensor_copy(rounded, product[:])
 
         def largest_square_norm(columns, result):
             squares = work.tile([P, PIECE], BF16, name="squares")
@@ -82,14 +87,15 @@ def tile_pagedattention_b_kernel(tc, kv, scale, q, offs, out):
         queries, keys, values_t, shift = [], [], [], []
         k_window, v_window, k_factors, v_factors = [], [], [], []
         for h in range(HEADS):
-            queries.append(held.tile([P, TOKENS], BF16, name="queries%d" % h))
-            nc.sync.dma_start(queries[h][:], q[h * P : (h + 1) * P, :])
             k_factors.append([load_factors(h * P, "k%d" % h, 0)])
             k_window.append(load_window(h * P, "k%d" % h))
+            queries.append(held.tile([P, TOKENS], BF16, name="queries%d" % h))
+            nc.sync.dma_start(queries[h][:], q[h * P : (h + 1) * P, :])
+            for p in range(1, PIECES):
+                k_factors[h].append(load_factors(h * P, "k%d" % h, p))
             v_factors.append([load_factors((HEADS + h) * P, "v%d" % h, 0)])
             v_window.append(load_window((HEADS + h) * P, "v%d" % h))
             for p in range(1, PIECES):
-                k_factors[h].append(load_factors(h * P, "k%d" % h, p))
                 v_factors[h].append(load_factors((HEADS + h) * P, "v%d" % h, p))
 
         q_norm, k_norm = [], []
@@ -101,16 +107,11 @@ def tile_pagedattention_b_kernel(tc, kv, scale, q, offs, out):
             k_norm.append(held.tile([P, PIECES], F32, name="k_norm%d" % h))
             nc.gpsimd.memset(values_t[h][:, :, P : P + 1], 1.0)
 
-        def measure_queries(h):
-            for p in range(PIECES):
-                largest_square_norm(queries[h][:, p * PIECE : (p + 1) * PIECE], q_norm[h][:, p : p + 1])
-
         def prepare_keys(h, p):
-            if p == 0:
-                measure_queries(h)
             piece = keys[h][:, p * PIECE : (p + 1) * PIECE]
             dequantise(k_window[h], k_factors[h][p], p, piece)
             largest_square_norm(piece, k_norm[h][:, p : p + 1])
+            largest_square_norm(queries[h][:, p * PIECE : (p + 1) * PIECE], q_norm[h][:, p : p + 1])
             seen = small.tile([P, 1], F32, name="seen")
             nc.vector.reduce_max(seen[:], k_norm[h][:, 0 : p + 1], axis=X)
             bound_sq = small.tile([P, 1], F32, name="bound_sq")
@@ -128,61 +129,70 @@ def tile_pagedattention_b_kernel(tc, kv, scale, q, offs, out):
             nc.vector.tensor_copy(values_t[h][:, p * PER : (p + 1) * PER, 0:P], flipped[:])
 
         chunks = [(h, c) for h in range(HEADS) for c in range(PIECES)]
-        prepare_keys(*chunks[0])
-        prepare_keys(*chunks[1])
-        prepare_values(*chunks[0])
-        for x in range(len(chunks)):
-            h, c = chunks[x]
-            out_t = [sums.tile([P, 2, P + 1], F32, name="out_t%d" % a) for a in range(PER // 2)]
-            normal = [None, None]
-            for jb in range(PER * (c + 1)):
-                first = max(jb - PER * c, 0)
-                lo = first * P
-                st = scores.tile([P, PIECE], F32, name="st")
-                nc.tensor.matmul(
-                    st[:, lo:],
-                    lhsT=keys[h][:, jb * P : (jb + 1) * P],
-                    rhs=queries[h][:, c * PIECE + lo : (c + 1) * PIECE],
-                    start=True,
-                    stop=True,
-                )
-                e = weights.tile([P, PIECE], BF16, name="e")
-                nc.scalar.activation(
-                    e[:, lo:], st[:, lo:], EXP, bias=shift[h][:, c : c + 1], scale=1.0 / math.sqrt(P)
-                )
-                if jb >= PER * c:
-                    nc.gpsimd.affine_select(
-                        out=e[:, lo : lo + P],
-                        in_=e[:, lo : lo + P],
-                        pattern=[[1, P]],
-                        compare_op=IS_GE,
-                        fill=0.0,
-                        base=0,
-                        channel_multiplier=-1,
-                    )
-                for r in range(first, PER):
-                    nc.tensor.matmul(
-                        out_t[r // 2][:, r % 2, :],
-                        lhsT=e[:, r * P : (r + 1) * P],
-                        rhs=values_t[h][:, jb, 0 : P + 1],
-                        start=(jb == 0 and r % 2 == 0),
-                        stop=(jb == PER * c + r and r % 2 == 1),
-                    )
-                if jb == 0:
-                    if x + 2 < len(chunks):
-                        prepare_keys(*chunks[x + 2])
-                    if x + 1 < len(chunks):
-                        prepare_values(*chunks[x + 1])
-                if jb >= PER * c and first % 2 == 1:
-                    a = first // 2
-                    inverse = small.tile([P, 2, 1], F32, name="inverse")
-                    nc.vector.reciprocal(inverse[:], out_t[a][:, :, P : P + 1])
-                    normal[a] = work.tile([P, 2, P], F32, name="normal")
-                    nc.vector.tensor_tensor(normal[a][:], out_t[a][:, :, 0:P], inverse[:].to_broadcast([P, 2, P]), MULT)
+        tiles = [(x, jb) for x in range(len(chunks)) for jb in range(PER * (chunks[x][1] + 1))]
+        LAG = 12
+        made = {}
+        sums_of = {}
 
-            turned = spare.tile([P, PIECE], F32, name="turned", tag="spare")
-            for r in range(PER):
-                nc.tensor.transpose(turned[:, r * P : (r + 1) * P], normal[r // 2][:, r % 2, :], ident_f[:])
-            staged = work.tile([P, PIECE], F32, name="staged")
-            nc.vector.tensor_copy(staged[:], turned[:])
-            nc.sync.dma_start(out[h * P : (h + 1) * P, c * PIECE : (c + 1) * PIECE], staged[:])
+        def front(x, jb):
+            h, c = chunks[x]
+            first = max(jb - PER * c, 0)
+            lo = first * P
+            st = scores.tile([P, PIECE], F32, name="st")
+            nc.tensor.matmul(
+                st[:, lo:],
+                lhsT=keys[h][:, jb * P : (jb + 1) * P],
+                rhs=queries[h][:, c * PIECE + lo : (c + 1) * PIECE],
+                start=True,
+                stop=True,
+            )
+            e = weights.tile([P, PIECE], BF16, name="e")
+            nc.scalar.activation(e[:, lo:], st[:, lo:], EXP, bias=shift[h][:, c : c + 1], scale=1.0 / math.sqrt(P))
+            if jb >= PER * c:
+                nc.vector.tensor_tensor(e[:, lo : lo + P], e[:, lo : lo + P], causal[:], MULT)
+            made[(x, jb)] = e
+
+        def back(x, jb):
+            h, c = chunks[x]
+            first = max(jb - PER * c, 0)
+            e = made[(x, jb)]
+            if jb == 0:
+                sums_of[x] = ([sums.tile([P, 2, P + 1], F32, name="out_t%d" % a) for a in range(PER // 2)], [None, None])
+            out_t, normal = sums_of[x]
+            for r in range(first, PER):
+                nc.tensor.matmul(
+                    out_t[r // 2][:, r % 2, :],
+                    lhsT=e[:, r * P : (r + 1) * P],
+                    rhs=values_t[h][:, jb, 0 : P + 1],
+                    start=(jb == 0 and r % 2 == 0),
+                    stop=(jb == PER * c + r and r % 2 == 1),
+                )
+            if jb >= PER * c and first % 2 == 1:
+                a = first // 2
+                inverse = small.tile([P, 2, 1], F32, name="inverse")
+                nc.vector.reciprocal(inverse[:], out_t[a][:, :, P : P + 1])
+                normal[a] = work.tile([P, 2, P], F32, name="normal")
+                nc.vector.tensor_tensor(normal[a][:], out_t[a][:, :, 0:P], inverse[:].to_broadcast([P, 2, P]), MULT)
+            if jb == PER * c + PER - 1:
+                turned = spare.tile([P, PIECE], F32, name="turned", tag="spare")
+                for r in range(PER):
+                    nc.tensor.transpose(turned[:, r * P : (r + 1) * P], normal[r // 2][:, r % 2, :], ident_f[:])
+                staged = work.tile([P, PIECE], F32, name="staged")
+                nc.vector.tensor_copy(staged[:], turned[:])
+                nc.sync.dma_start(out[h * P : (h + 1) * P, c * PIECE : (c + 1) * PIECE], staged[:])
+
+        for x in range(PIECES):
+            prepare_keys(*chunks[x])
+        prepare_values(*chunks[0])
+        todo = [(prepare_values, x) for x in range(1, PIECES)]
+        for x in range(PIECES, len(chunks)):
+            todo.append((prepare_keys, x))
+            todo.append((prepare_values, x))
+        for n in range(len(tiles) + LAG):
+            if n < len(tiles):
+                front(*tiles[n])
+            if n >= LAG:
+                back(*tiles[n - LAG])
+            if n % 3 == 0 and n // 3 < len(todo):
+                prepare, x = todo[n // 3]
+                prepare(*chunks[x])

@@ -178,7 +178,7 @@ def tile_pagedattention_b_kernel(tc, kv, scale, q, offs, out):
                 for r in range(PER):
                     nc.tensor.transpose(turned[:, r * P : (r + 1) * P], normal[r // 2][:, r % 2, :], ident_f[:])
                 staged = work.tile([P, PIECE], F32, name="staged")
-                nc.vector.tensor_copy(staged[:], turned[:])
+                nc.scalar.copy(staged[:], turned[:])
                 nc.sync.dma_start(out[h * P : (h + 1) * P, c * PIECE : (c + 1) * PIECE], staged[:])
 
         for x in range(PIECES):

@@ -10,6 +10,7 @@ MULT = mybir.AluOpType.mult
 POW = mybir.AluOpType.pow
 IS_GE = mybir.AluOpType.is_ge
 EXP = mybir.ActivationFunctionType.Exp
+COPY = mybir.ActivationFunctionType.Copy
 X = mybir.AxisListType.X
 
 P = 128
@@ -22,9 +23,10 @@ BLOCKS = TOKENS // P
 PER = PIECE // P
 VROW = 144
 SLACK = 1.02
+LAG = PER + 2 * PER
 
 FLOPS = HEADS * 2 * 2 * P * (TOKENS * (TOKENS + 1) // 2)
-BYTES = 4 * P * TOKENS * 4 * 2 + HEADS * P * TOKENS * (2 + 4) + TOKENS * 2
+BYTES = 2 * HEADS * P * TOKENS * (4 + 4) + HEADS * P * TOKENS * (2 + 4) + TOKENS * 2
 
 
 def tile_pagedattention_b_kernel(tc, kv, scale, q, offs, out):
@@ -34,7 +36,7 @@ def tile_pagedattention_b_kernel(tc, kv, scale, q, offs, out):
         tc.tile_pool(name="work", bufs=3) as work,
         tc.tile_pool(name="prod", bufs=2) as prod,
         tc.tile_pool(name="small", bufs=4) as small,
-        tc.tile_pool(name="weights", bufs=16) as weights,
+        tc.tile_pool(name="weights", bufs=LAG + 4) as weights,
         tc.psum_pool(name="scores", bufs=3) as scores,
         tc.psum_pool(name="sums", bufs=2) as sums,
         tc.psum_pool(name="spare", bufs=1) as spare,
@@ -56,18 +58,37 @@ def tile_pagedattention_b_kernel(tc, kv, scale, q, offs, out):
         half = held.tile([P, 1], F32, name="half")
         nc.gpsimd.memset(half[:], 0.5)
 
-        SLAB = SLOTS // 4
-
         def load_window(row, name):
             window = held.tile([P, SLOTS], F32, name="window_" + name)
-            for s in range(0, SLOTS, SLAB):
-                nc.sync.dma_start(window[:, s : s + SLAB], kv[row : row + P, s : s + SLAB])
+            nc.sync.dma_start(window[:], kv[row : row + P, :])
             return window
 
         def load_factors(row, name, p):
             factors = held.tile([P, PIECE], F32, name="factors_%s%d" % (name, p))
             nc.sync.dma_start(factors[:], scale[row : row + P, p * PIECE : (p + 1) * PIECE])
             return factors
+
+        queries, k_window, v_window, k_factors, v_factors = [], [], [], [], []
+        for h in range(HEADS):
+            k_factors.append([load_factors(h * P, "k%d" % h, 0)])
+            k_window.append(load_window(h * P, "k%d" % h))
+            queries.append(held.tile([P, TOKENS], BF16, name="queries%d" % h))
+            nc.sync.dma_start(queries[h][:], q[h * P : (h + 1) * P, :])
+            for p in range(1, PIECES):
+                k_factors[h].append(load_factors(h * P, "k%d" % h, p))
+            v_factors.append([load_factors((HEADS + h) * P, "v%d" % h, 0)])
+            v_window.append(load_window((HEADS + h) * P, "v%d" % h))
+            for p in range(1, PIECES):
+                v_factors[h].append(load_factors((HEADS + h) * P, "v%d" % h, p))
+
+        keys, values_t, shift, q_norm, k_norm = [], [], [], [], []
+        for h in range(HEADS):
+            keys.append(held.tile([P, TOKENS], BF16, name="keys%d" % h))
+            values_t.append(held.tile([P, BLOCKS, VROW], BF16, name="values_t%d" % h))
+            shift.append(held.tile([P, PIECES], F32, name="shift%d" % h))
+            q_norm.append(held.tile([P, PIECES], F32, name="q_norm%d" % h))
+            k_norm.append(held.tile([P, PIECES], F32, name="k_norm%d" % h))
+            nc.gpsimd.memset(values_t[h][:, :, P : P + 1], 1.0)
 
         def dequantise(window, factors, p, rounded):
             wide = PIECE // 16
@@ -83,29 +104,6 @@ def tile_pagedattention_b_kernel(tc, kv, scale, q, offs, out):
             norms = spare.tile([P, PIECE], F32, name="norms", tag="spare")
             nc.tensor.matmul(norms[:], lhsT=ones[:], rhs=squares[:], start=True, stop=True)
             nc.vector.reduce_max(result, norms[:], axis=X)
-
-        queries, keys, values_t, shift = [], [], [], []
-        k_window, v_window, k_factors, v_factors = [], [], [], []
-        for h in range(HEADS):
-            k_factors.append([load_factors(h * P, "k%d" % h, 0)])
-            k_window.append(load_window(h * P, "k%d" % h))
-            queries.append(held.tile([P, TOKENS], BF16, name="queries%d" % h))
-            nc.sync.dma_start(queries[h][:], q[h * P : (h + 1) * P, :])
-            for p in range(1, PIECES):
-                k_factors[h].append(load_factors(h * P, "k%d" % h, p))
-            v_factors.append([load_factors((HEADS + h) * P, "v%d" % h, 0)])
-            v_window.append(load_window((HEADS + h) * P, "v%d" % h))
-            for p in range(1, PIECES):
-                v_factors[h].append(load_factors((HEADS + h) * P, "v%d" % h, p))
-
-        q_norm, k_norm = [], []
-        for h in range(HEADS):
-            keys.append(held.tile([P, TOKENS], BF16, name="keys%d" % h))
-            values_t.append(held.tile([P, BLOCKS, VROW], BF16, name="values_t%d" % h))
-            shift.append(held.tile([P, PIECES], F32, name="shift%d" % h))
-            q_norm.append(held.tile([P, PIECES], F32, name="q_norm%d" % h))
-            k_norm.append(held.tile([P, PIECES], F32, name="k_norm%d" % h))
-            nc.gpsimd.memset(values_t[h][:, :, P : P + 1], 1.0)
 
         def prepare_keys(h, p):
             piece = keys[h][:, p * PIECE : (p + 1) * PIECE]
@@ -126,15 +124,14 @@ def tile_pagedattention_b_kernel(tc, kv, scale, q, offs, out):
             flipped = spare.tile([P, PER, P], BF16, name="flipped", tag="spare")
             for k in range(PER):
                 nc.tensor.transpose(flipped[:, k, :], values[:, k * P : (k + 1) * P], ident_bf[:])
-            nc.vector.tensor_copy(values_t[h][:, p * PER : (p + 1) * PER, 0:P], flipped[:])
+            nc.scalar.copy(values_t[h][:, p * PER : (p + 1) * PER, 0:P], flipped[:])
 
         chunks = [(h, c) for h in range(HEADS) for c in range(PIECES)]
         tiles = [(x, jb) for x in range(len(chunks)) for jb in range(PER * (chunks[x][1] + 1))]
-        LAG = 12
         made = {}
         sums_of = {}
 
-        def front(x, jb):
+        def scores_and_weights(x, jb):
             h, c = chunks[x]
             first = max(jb - PER * c, 0)
             lo = first * P
@@ -152,7 +149,7 @@ def tile_pagedattention_b_kernel(tc, kv, scale, q, offs, out):
                 nc.vector.tensor_tensor(e[:, lo : lo + P], e[:, lo : lo + P], causal[:], MULT)
             made[(x, jb)] = e
 
-        def back(x, jb):
+        def weighted_sums(x, jb):
             h, c = chunks[x]
             first = max(jb - PER * c, 0)
             e = made[(x, jb)]
@@ -172,7 +169,8 @@ def tile_pagedattention_b_kernel(tc, kv, scale, q, offs, out):
                 inverse = small.tile([P, 2, 1], F32, name="inverse")
                 nc.vector.reciprocal(inverse[:], out_t[a][:, :, P : P + 1])
                 normal[a] = work.tile([P, 2, P], F32, name="normal")
-                nc.vector.tensor_tensor(normal[a][:], out_t[a][:, :, 0:P], inverse[:].to_broadcast([P, 2, P]), MULT)
+                for b in range(2):
+                    nc.scalar.activation(normal[a][:, b, :], out_t[a][:, b, 0:P], COPY, scale=inverse[:, b, :])
             if jb == PER * c + PER - 1:
                 turned = spare.tile([P, PIECE], F32, name="turned", tag="spare")
                 for r in range(PER):
@@ -184,15 +182,19 @@ def tile_pagedattention_b_kernel(tc, kv, scale, q, offs, out):
         for x in range(PIECES):
             prepare_keys(*chunks[x])
         prepare_values(*chunks[0])
-        todo = [(prepare_values, x) for x in range(1, PIECES)]
+        later = [("values", x) for x in range(1, PIECES)]
         for x in range(PIECES, len(chunks)):
-            todo.append((prepare_keys, x))
-            todo.append((prepare_values, x))
+            later.append(("keys", x))
+            later.append(("values", x))
+        STEP = len(tiles) // HEADS // len(later)
         for n in range(len(tiles) + LAG):
             if n < len(tiles):
-                front(*tiles[n])
+                scores_and_weights(*tiles[n])
             if n >= LAG:
-                back(*tiles[n - LAG])
-            if n % 3 == 0 and n // 3 < len(todo):
-                prepare, x = todo[n // 3]
-                prepare(*chunks[x])
+                weighted_sums(*tiles[n - LAG])
+            if n % STEP == 0 and n // STEP < len(later):
+                what, x = later[n // STEP]
+                if what == "keys":
+                    prepare_keys(*chunks[x])
+                else:
+                    prepare_values(*chunks[x])

@@ -23,6 +23,8 @@ BLOCKS = TOKENS // P
 PER = PIECE // P
 VROW = 144
 SLACK = 1.02
+STEP = 4
+AHEAD = 2
 LAG = PER + 2 * PER
 
 FLOPS = HEADS * 2 * 2 * P * (TOKENS * (TOKENS + 1) // 2)
@@ -33,13 +35,12 @@ def tile_pagedattention_b_kernel(tc, kv, scale, q, offs, out):
     nc = tc.nc
     with (
         tc.tile_pool(name="held", bufs=1) as held,
-        tc.tile_pool(name="work", bufs=3) as work,
-        tc.tile_pool(name="prod", bufs=2) as prod,
+        tc.tile_pool(name="work", bufs=4) as work,
+        tc.tile_pool(name="prep", bufs=3) as prep,
         tc.tile_pool(name="small", bufs=4) as small,
         tc.tile_pool(name="weights", bufs=LAG + 4) as weights,
-        tc.psum_pool(name="scores", bufs=3) as scores,
+        tc.psum_pool(name="scores", bufs=4) as scores,
         tc.psum_pool(name="sums", bufs=2) as sums,
-        tc.psum_pool(name="spare", bufs=1) as spare,
     ):
         offsets = held.tile([P, TOKENS // 16], U16, name="offsets")
         nc.sync.dma_start(offsets[:], offs)
@@ -55,8 +56,10 @@ def tile_pagedattention_b_kernel(tc, kv, scale, q, offs, out):
         nc.gpsimd.affine_select(
             out=causal[:], in_=causal[:], pattern=[[1, P]], compare_op=IS_GE, fill=0.0, base=0, channel_multiplier=-1
         )
-        half = held.tile([P, 1], F32, name="half")
+        half = held.tile([P, PIECES], F32, name="half")
         nc.gpsimd.memset(half[:], 0.5)
+        warm = held.tile([P, 1], F32, name="warm")
+        nc.scalar.activation(warm[:], half[:, 0:1], EXP)
 
         def load_window(row, name):
             window = held.tile([P, SLOTS], F32, name="window_" + name)
@@ -70,10 +73,11 @@ def tile_pagedattention_b_kernel(tc, kv, scale, q, offs, out):
 
         queries, k_window, v_window, k_factors, v_factors = [], [], [], [], []
         for h in range(HEADS):
-            k_factors.append([load_factors(h * P, "k%d" % h, 0)])
-            k_window.append(load_window(h * P, "k%d" % h))
             queries.append(held.tile([P, TOKENS], BF16, name="queries%d" % h))
             nc.sync.dma_start(queries[h][:], q[h * P : (h + 1) * P, :])
+        for h in range(HEADS):
+            k_factors.append([load_factors(h * P, "k%d" % h, 0)])
+            k_window.append(load_window(h * P, "k%d" % h))
             for p in range(1, PIECES):
                 k_factors[h].append(load_factors(h * P, "k%d" % h, p))
             v_factors.append([load_factors((HEADS + h) * P, "v%d" % h, 0)])
@@ -81,55 +85,89 @@ def tile_pagedattention_b_kernel(tc, kv, scale, q, offs, out):
             for p in range(1, PIECES):
                 v_factors[h].append(load_factors((HEADS + h) * P, "v%d" % h, p))
 
-        keys, values_t, shift, q_norm, k_norm = [], [], [], [], []
+        keys, values_t, shift, q_norm, q_factor, k_norm = [], [], [], [], [], []
         for h in range(HEADS):
             keys.append(held.tile([P, TOKENS], BF16, name="keys%d" % h))
             values_t.append(held.tile([P, BLOCKS, VROW], BF16, name="values_t%d" % h))
             shift.append(held.tile([P, PIECES], F32, name="shift%d" % h))
             q_norm.append(held.tile([P, PIECES], F32, name="q_norm%d" % h))
+            q_factor.append(held.tile([P, PIECES], F32, name="q_factor%d" % h))
             k_norm.append(held.tile([P, PIECES], F32, name="k_norm%d" % h))
             nc.gpsimd.memset(values_t[h][:, :, P : P + 1], 1.0)
 
         def dequantise(window, factors, p, rounded):
             wide = PIECE // 16
-            product = prod.tile([P, PIECE], F32, name="product")
+            product = prep.tile([P, PIECE], F32, name="product", tag="prep")
             nc.vector.tensor_tensor(
                 product[:], window[:].indirect(offsets[:, p * wide : (p + 1) * wide]), factors[:], MULT
             )
+            if rounded is None:
+                values = prep.tile([P, PIECE], BF16, name="values", tag="prep")
+                rounded = values[:]
             nc.vector.tensor_copy(rounded, product[:])
+            return rounded
 
-        def largest_square_norm(columns, result):
-            squares = work.tile([P, PIECE], BF16, name="squares")
+        passed = {}
+
+        def query_norms(h, c):
+            squares = prep.tile([P, PIECE], BF16, name="q_squares", tag="prep")
+            columns = queries[h][:, c * PIECE : (c + 1) * PIECE]
             nc.vector.tensor_tensor(squares[:], columns, columns, MULT)
-            norms = spare.tile([P, PIECE], F32, name="norms", tag="spare")
+            norms = scores.tile([P, PIECE], F32, name="q_norms", tag="st")
             nc.tensor.matmul(norms[:], lhsT=ones[:], rhs=squares[:], start=True, stop=True)
-            nc.vector.reduce_max(result, norms[:], axis=X)
+            nc.vector.reduce_max(q_norm[h][:, c : c + 1], norms[:], axis=X)
 
-        def prepare_keys(h, p):
+        def query_factors(h):
+            q_root = small.tile([P, PIECES], F32, name="q_root")
+            nc.gpsimd.tensor_tensor(q_root[:], q_norm[h][:], half[:], POW)
+            nc.gpsimd.tensor_scalar(q_factor[h][:], q_root[:], -math.sqrt(SLACK / P), None, op0=MULT)
+
+        def keys_gather(h, p):
             piece = keys[h][:, p * PIECE : (p + 1) * PIECE]
             dequantise(k_window[h], k_factors[h][p], p, piece)
-            largest_square_norm(piece, k_norm[h][:, p : p + 1])
-            largest_square_norm(queries[h][:, p * PIECE : (p + 1) * PIECE], q_norm[h][:, p : p + 1])
-            seen = small.tile([P, 1], F32, name="seen")
-            nc.vector.reduce_max(seen[:], k_norm[h][:, 0 : p + 1], axis=X)
-            bound_sq = small.tile([P, 1], F32, name="bound_sq")
-            nc.vector.tensor_scalar(bound_sq[:], seen[:], q_norm[h][:, p : p + 1], SLACK / P, op0=MULT, op1=MULT)
-            bound = small.tile([P, 1], F32, name="bound")
-            nc.gpsimd.tensor_tensor(bound[:], bound_sq[:], half[:], POW)
-            nc.gpsimd.tensor_scalar(shift[h][:, p : p + 1], bound[:], -1.0, None, op0=MULT)
+            squares = prep.tile([P, PIECE], BF16, name="squares", tag="prep")
+            nc.vector.tensor_tensor(squares[:], piece, piece, MULT)
+            passed[("squares", h, p)] = squares
 
-        def prepare_values(h, p):
-            values = work.tile([P, PIECE], BF16, name="values")
-            dequantise(v_window[h], v_factors[h][p], p, values[:])
-            flipped = spare.tile([P, PER, P], BF16, name="flipped", tag="spare")
+        def keys_column_sums(h, p):
+            norms = scores.tile([P, PIECE], F32, name="norms", tag="st")
+            nc.tensor.matmul(norms[:], lhsT=ones[:], rhs=passed[("squares", h, p)][:], start=True, stop=True)
+            passed[("norms", h, p)] = norms
+
+        def keys_shift(h, p):
+            nc.vector.reduce_max(k_norm[h][:, p : p + 1], passed[("norms", h, p)][:], axis=X)
+            seen = k_norm[h][:, 0:1]
+            if p > 0:
+                seen_so_far = small.tile([P, 1], F32, name="seen_so_far")
+                nc.vector.reduce_max(seen_so_far[:], k_norm[h][:, 0 : p + 1], axis=X)
+                seen = seen_so_far[:]
+            k_root = small.tile([P, 1], F32, name="k_root")
+            nc.gpsimd.tensor_tensor(k_root[:], seen, half[:, 0:1], POW)
+            nc.gpsimd.tensor_tensor(shift[h][:, p : p + 1], k_root[:], q_factor[h][:, p : p + 1], MULT)
+
+        def values_gather(h, p):
+            passed[("values", h, p)] = dequantise(v_window[h], v_factors[h][p], p, None)
+
+        def values_flip(h, p):
+            flipped = scores.tile([P, PER, P], BF16, name="flipped", tag="st")
             for k in range(PER):
-                nc.tensor.transpose(flipped[:, k, :], values[:, k * P : (k + 1) * P], ident_bf[:])
-            nc.scalar.copy(values_t[h][:, p * PER : (p + 1) * PER, 0:P], flipped[:])
+                nc.tensor.transpose(flipped[:, k, :], passed[("values", h, p)][:, k * P : (k + 1) * P], ident_bf[:])
+            passed[("flipped", h, p)] = flipped
+
+        def values_keep(h, p):
+            nc.scalar.copy(values_t[h][:, p * PER : (p + 1) * PER, 0:P], passed[("flipped", h, p)][:])
+
+        KEYS_STAGES = ((0, keys_gather), (3, keys_column_sums), (4, keys_shift))
+        VALUES_STAGES = ((0, values_gather), (3, values_flip), (4, values_keep))
 
         chunks = [(h, c) for h in range(HEADS) for c in range(PIECES)]
         tiles = [(x, jb) for x in range(len(chunks)) for jb in range(PER * (chunks[x][1] + 1))]
         made = {}
         sums_of = {}
+        agenda = {}
+
+        def write_at(step, call, *args):
+            agenda.setdefault(step, []).append((call, args))
 
         def scores_and_weights(x, jb):
             h, c = chunks[x]
@@ -149,13 +187,40 @@ def tile_pagedattention_b_kernel(tc, kv, scale, q, offs, out):
                 nc.vector.tensor_tensor(e[:, lo : lo + P], e[:, lo : lo + P], causal[:], MULT)
             made[(x, jb)] = e
 
-        def weighted_sums(x, jb):
+        def normalise(x, a):
+            h, c = chunks[x]
+            out_t, normal, inverse = sums_of[x]
+            normal[a] = work.tile([P, 2, P], F32, name="normal")
+            for b in range(2):
+                if h == 0:
+                    nc.scalar.activation(normal[a][:, b, :], out_t[a][:, b, 0:P], COPY, scale=inverse[a][:, b, :])
+                else:
+                    nc.vector.tensor_scalar(normal[a][:, b, :], out_t[a][:, b, 0:P], inverse[a][:, b, :], None, op0=MULT)
+
+        def turn(x):
+            normal = sums_of[x][1]
+            turned = scores.tile([P, PIECE], F32, name="turned", tag="st")
+            for r in range(PER):
+                nc.tensor.transpose(turned[:, r * P : (r + 1) * P], normal[r // 2][:, r % 2, :], ident_f[:])
+            passed[("turned", x)] = turned
+
+        def store(x):
+            h, c = chunks[x]
+            staged = work.tile([P, PIECE], F32, name="staged")
+            if h == 0:
+                nc.scalar.copy(staged[:], passed[("turned", x)][:])
+            else:
+                nc.vector.tensor_copy(staged[:], passed[("turned", x)][:])
+            nc.sync.dma_start(out[h * P : (h + 1) * P, c * PIECE : (c + 1) * PIECE], staged[:])
+
+        def weighted_sums(x, jb, step):
             h, c = chunks[x]
             first = max(jb - PER * c, 0)
             e = made[(x, jb)]
             if jb == 0:
-                sums_of[x] = ([sums.tile([P, 2, P + 1], F32, name="out_t%d" % a) for a in range(PER // 2)], [None, None])
-            out_t, normal = sums_of[x]
+                out_t = [sums.tile([P, 2, P + 1], F32, name="out_t%d" % a) for a in range(PER // 2)]
+                sums_of[x] = (out_t, [None, None], [None, None])
+            out_t, normal, inverse = sums_of[x]
             for r in range(first, PER):
                 nc.tensor.matmul(
                     out_t[r // 2][:, r % 2, :],
@@ -166,35 +231,31 @@ def tile_pagedattention_b_kernel(tc, kv, scale, q, offs, out):
                 )
             if jb >= PER * c and first % 2 == 1:
                 a = first // 2
-                inverse = small.tile([P, 2, 1], F32, name="inverse")
-                nc.vector.reciprocal(inverse[:], out_t[a][:, :, P : P + 1])
-                normal[a] = work.tile([P, 2, P], F32, name="normal")
-                for b in range(2):
-                    nc.scalar.activation(normal[a][:, b, :], out_t[a][:, b, 0:P], COPY, scale=inverse[:, b, :])
+                inverse[a] = small.tile([P, 2, 1], F32, name="inverse")
+                nc.vector.reciprocal(inverse[a][:], out_t[a][:, :, P : P + 1])
+                write_at(step + 1, normalise, x, a)
             if jb == PER * c + PER - 1:
-                turned = spare.tile([P, PIECE], F32, name="turned", tag="spare")
-                for r in range(PER):
-                    nc.tensor.transpose(turned[:, r * P : (r + 1) * P], normal[r // 2][:, r % 2, :], ident_f[:])
-                staged = work.tile([P, PIECE], F32, name="staged")
-                nc.scalar.copy(staged[:], turned[:])
-                nc.sync.dma_start(out[h * P : (h + 1) * P, c * PIECE : (c + 1) * PIECE], staged[:])
+                write_at(step + 3, turn, x)
+                write_at(step + 4, store, x)
 
-        for x in range(PIECES):
-            prepare_keys(*chunks[x])
-        prepare_values(*chunks[0])
-        later = [("values", x) for x in range(1, PIECES)]
-        for x in range(PIECES, len(chunks)):
-            later.append(("keys", x))
-            later.append(("values", x))
-        STEP = len(tiles) // HEADS // len(later)
-        for n in range(len(tiles) + LAG):
-            if n < len(tiles):
+        for h in range(HEADS):
+            for c in range(PIECES):
+                query_norms(h, c)
+            query_factors(h)
+        preparations = []
+        for h in range(HEADS):
+            for stages, p in ((KEYS_STAGES, 0), (KEYS_STAGES, 1), (KEYS_STAGES, 2), (VALUES_STAGES, 0), (KEYS_STAGES, 3)):
+                preparations.append((stages, h, p))
+            preparations.extend([(VALUES_STAGES, h, p) for p in range(1, PIECES)])
+        for k in range(len(preparations)):
+            stages, h, p = preparations[k]
+            for wait, call in stages:
+                write_at((k - AHEAD) * STEP + wait, call, h, p)
+        LAST = 4
+        for n in range(-AHEAD * STEP, len(tiles) + LAG + LAST):
+            if 0 <= n < len(tiles):
                 scores_and_weights(*tiles[n])
-            if n >= LAG:
-                weighted_sums(*tiles[n - LAG])
-            if n % STEP == 0 and n // STEP < len(later):
-                what, x = later[n // STEP]
-                if what == "keys":
-                    prepare_keys(*chunks[x])
-                else:
-                    prepare_values(*chunks[x])
+            if LAG <= n < len(tiles) + LAG:
+                weighted_sums(*tiles[n - LAG], n)
+            for call, args in agenda.get(n, []):
+                call(*args)

@@ -7,6 +7,7 @@ F32 = mybir.dt.float32
 BF16 = mybir.dt.bfloat16
 U16 = mybir.dt.uint16
 MULT = mybir.AluOpType.mult
+MAX = mybir.AluOpType.max
 POW = mybir.AluOpType.pow
 IS_GE = mybir.AluOpType.is_ge
 EXP = mybir.ActivationFunctionType.Exp
@@ -109,13 +110,17 @@ def tile_pagedattention_b_kernel(tc, kv, scale, q, offs, out):
 
         passed = {}
 
+        def largest(norms, result):
+            spent = work.tile([P, PIECE], BF16, name="spent")
+            nc.vector.tensor_scalar(spent[:], norms[:], 1.0, None, op0=MULT, op1=MAX, accum_out=result)
+
         def query_norms(h, c):
             squares = prep.tile([P, PIECE], BF16, name="q_squares", tag="prep")
             columns = queries[h][:, c * PIECE : (c + 1) * PIECE]
             nc.vector.tensor_tensor(squares[:], columns, columns, MULT)
-            norms = scores.tile([P, PIECE], F32, name="q_norms", tag="st")
+            norms = scores.tile([P, PIECE], BF16, name="q_norms", tag="st")
             nc.tensor.matmul(norms[:], lhsT=ones[:], rhs=squares[:], start=True, stop=True)
-            nc.vector.reduce_max(q_norm[h][:, c : c + 1], norms[:], axis=X)
+            largest(norms, q_norm[h][:, c : c + 1])
 
         def query_factors(h):
             q_root = small.tile([P, PIECES], F32, name="q_root")
@@ -130,12 +135,12 @@ def tile_pagedattention_b_kernel(tc, kv, scale, q, offs, out):
             passed[("squares", h, p)] = squares
 
         def keys_column_sums(h, p):
-            norms = scores.tile([P, PIECE], F32, name="norms", tag="st")
+            norms = scores.tile([P, PIECE], BF16, name="norms", tag="st")
             nc.tensor.matmul(norms[:], lhsT=ones[:], rhs=passed[("squares", h, p)][:], start=True, stop=True)
             passed[("norms", h, p)] = norms
 
         def keys_shift(h, p):
-            nc.vector.reduce_max(k_norm[h][:, p : p + 1], passed[("norms", h, p)][:], axis=X)
+            largest(passed[("norms", h, p)], k_norm[h][:, p : p + 1])
             seen = k_norm[h][:, 0:1]
             if p > 0:
                 seen_so_far = small.tile([P, 1], F32, name="seen_so_far")
@@ -155,7 +160,7 @@ def tile_pagedattention_b_kernel(tc, kv, scale, q, offs, out):
             passed[("flipped", h, p)] = flipped
 
         def values_keep(h, p):
-            nc.scalar.copy(values_t[h][:, p * PER : (p + 1) * PER, 0:P], passed[("flipped", h, p)][:])
+            nc.vector.tensor_copy(values_t[h][:, p * PER : (p + 1) * PER, 0:P], passed[("flipped", h, p)][:])
 
         KEYS_STAGES = ((0, keys_gather), (3, keys_column_sums), (4, keys_shift))
         VALUES_STAGES = ((0, values_gather), (3, values_flip), (4, values_keep))

@@ -40,6 +40,7 @@ def tile_pagedattention_b_kernel(tc, kv, scale, q, offs, out):
         tc.tile_pool(name="prep", bufs=3) as prep,
         tc.tile_pool(name="small", bufs=4) as small,
         tc.tile_pool(name="weights", bufs=LAG + 4) as weights,
+        tc.tile_pool(name="stairs", bufs=3) as stairs_pool,
         tc.psum_pool(name="scores", bufs=4) as scores,
         tc.psum_pool(name="sums", bufs=2) as sums,
     ):
@@ -186,21 +187,28 @@ def tile_pagedattention_b_kernel(tc, kv, scale, q, offs, out):
                 start=True,
                 stop=True,
             )
-            e = weights.tile([P, PIECE], BF16, name="e")
-            nc.scalar.activation(e[:, lo:], st[:, lo:], EXP, bias=shift[h][:, c : c + 1], scale=1.0 / math.sqrt(P))
-            if jb >= PER * c:
-                nc.vector.tensor_tensor(e[:, lo : lo + P], e[:, lo : lo + P], causal[:], MULT)
+            if jb < PER * c:
+                whole = weights.tile([P, PIECE], BF16, name="e")
+                e = whole[:]
+            else:
+                if first == 0:
+                    passed[("stairs", x)] = stairs_pool.tile([P, PER, PIECE], BF16, name="stairs")
+                e = passed[("stairs", x)][:, first, 0 : PIECE - lo]
+            nc.scalar.activation(e, st[:, lo:], EXP, bias=shift[h][:, c : c + 1], scale=1.0 / math.sqrt(P))
+            if first == PER - 1:
+                on_diagonal = passed[("stairs", x)][:, :, 0:P]
+                nc.vector.tensor_tensor(on_diagonal, on_diagonal, causal[:].unsqueeze(1).to_broadcast([P, PER, P]), MULT)
             made[(x, jb)] = e
 
         def normalise(x, a):
             h, c = chunks[x]
             out_t, normal, inverse = sums_of[x]
             normal[a] = work.tile([P, 2, P], F32, name="normal")
-            for b in range(2):
-                if h == 0:
+            if h == 0:
+                for b in range(2):
                     nc.scalar.activation(normal[a][:, b, :], out_t[a][:, b, 0:P], COPY, scale=inverse[a][:, b, :])
-                else:
-                    nc.vector.tensor_scalar(normal[a][:, b, :], out_t[a][:, b, 0:P], inverse[a][:, b, :], None, op0=MULT)
+            else:
+                nc.vector.tensor_tensor(normal[a][:], out_t[a][:, :, 0:P], inverse[a][:].to_broadcast([P, 2, P]), MULT)
 
         def turn(x):
             normal = sums_of[x][1]
@@ -229,7 +237,7 @@ def tile_pagedattention_b_kernel(tc, kv, scale, q, offs, out):
             for r in range(first, PER):
                 nc.tensor.matmul(
                     out_t[r // 2][:, r % 2, :],
-                    lhsT=e[:, r * P : (r + 1) * P],
+                    lhsT=e[:, (r - first) * P : (r - first + 1) * P],
                     rhs=values_t[h][:, jb, 0 : P + 1],
                     start=(jb == 0 and r % 2 == 0),
                     stop=(jb == PER * c + r and r % 2 == 1),

@@ -163,8 +163,8 @@ def tile_pagedattention_b_kernel(tc, kv, scale, q, offs, out):
         def values_keep(h, p):
             nc.vector.tensor_copy(values_t[h][:, p * PER : (p + 1) * PER, 0:P], passed[("flipped", h, p)][:])
 
-        KEYS_STAGES = ((0, keys_gather), (3, keys_column_sums), (4, keys_shift))
-        VALUES_STAGES = ((0, values_gather), (3, values_flip), (4, values_keep))
+        KEYS_STAGES = ((0, keys_gather), (6, keys_column_sums), (7, keys_shift))
+        VALUES_STAGES = ((0, values_gather), (6, values_flip), (7, values_keep))
 
         chunks = [(h, c) for h in range(HEADS) for c in range(PIECES)]
         tiles = [(x, jb) for x in range(len(chunks)) for jb in range(PER * (chunks[x][1] + 1))]
@@ -210,21 +210,22 @@ def tile_pagedattention_b_kernel(tc, kv, scale, q, offs, out):
             else:
                 nc.vector.tensor_tensor(normal[a][:], out_t[a][:, :, 0:P], inverse[a][:].to_broadcast([P, 2, P]), MULT)
 
-        def turn(x):
+        def turn(x, a):
             normal = sums_of[x][1]
-            turned = scores.tile([P, PIECE], F32, name="turned", tag="st")
-            for r in range(PER):
-                nc.tensor.transpose(turned[:, r * P : (r + 1) * P], normal[r // 2][:, r % 2, :], ident_f[:])
-            passed[("turned", x)] = turned
+            turned = scores.tile([P, 2 * P], F32, name="turned", tag="st")
+            for b in range(2):
+                nc.tensor.transpose(turned[:, b * P : (b + 1) * P], normal[a][:, b, :], ident_f[:])
+            passed[("turned", x, a)] = turned
 
-        def store(x):
+        def store(x, a):
             h, c = chunks[x]
-            staged = work.tile([P, PIECE], F32, name="staged")
+            staged = work.tile([P, 2 * P], F32, name="staged")
             if h == 0:
-                nc.scalar.copy(staged[:], passed[("turned", x)][:])
+                nc.scalar.copy(staged[:], passed[("turned", x, a)][:])
             else:
-                nc.vector.tensor_copy(staged[:], passed[("turned", x)][:])
-            nc.sync.dma_start(out[h * P : (h + 1) * P, c * PIECE : (c + 1) * PIECE], staged[:])
+                nc.vector.tensor_copy(staged[:], passed[("turned", x, a)][:])
+            lo = c * PIECE + a * 2 * P
+            nc.sync.dma_start(out[h * P : (h + 1) * P, lo : lo + 2 * P], staged[:])
 
         def weighted_sums(x, jb, step):
             h, c = chunks[x]
@@ -247,9 +248,8 @@ def tile_pagedattention_b_kernel(tc, kv, scale, q, offs, out):
                 inverse[a] = small.tile([P, 2, 1], F32, name="inverse")
                 nc.vector.reciprocal(inverse[a][:], out_t[a][:, :, P : P + 1])
                 write_at(step + 1, normalise, x, a)
-            if jb == PER * c + PER - 1:
-                write_at(step + 3, turn, x)
-                write_at(step + 4, store, x)
+                write_at(step + 3, turn, x, a)
+                write_at(step + 4, store, x, a)
 
         for h in range(HEADS):
             for c in range(PIECES):

@@ -41,8 +41,8 @@ def tile_pagedattention_b_kernel(tc, kv, scale, q, offs, out):
         tc.tile_pool(name="small", bufs=4) as small,
         tc.tile_pool(name="weights", bufs=LAG + 4) as weights,
         tc.tile_pool(name="stairs", bufs=3) as stairs_pool,
-        tc.psum_pool(name="scores", bufs=4) as scores,
-        tc.psum_pool(name="sums", bufs=2) as sums,
+        tc.psum_pool(name="scores", bufs=5) as scores,
+        tc.psum_pool(name="sums", bufs=3) as sums,
     ):
         offsets = held.tile([P, TOKENS // 16], U16, name="offsets")
         nc.sync.dma_start(offsets[:], offs)
@@ -232,7 +232,7 @@ def tile_pagedattention_b_kernel(tc, kv, scale, q, offs, out):
             first = max(jb - PER * c, 0)
             e = made[(x, jb)]
             if jb == 0:
-                out_t = [sums.tile([P, 2, P + 1], F32, name="out_t%d" % a) for a in range(PER // 2)]
+                out_t = [sums.tile([P, 2, P + 1], F32, name="out_t%d" % a, tag="out_t") for a in range(PER // 2)]
                 sums_of[x] = (out_t, [None, None], [None, None])
             out_t, normal, inverse = sums_of[x]
             for r in range(first, PER):

@@ -7,12 +7,11 @@ F32 = mybir.dt.float32
 BF16 = mybir.dt.bfloat16
 U16 = mybir.dt.uint16
 MULT = mybir.AluOpType.mult
-MAX = mybir.AluOpType.max
-POW = mybir.AluOpType.pow
+ADD = mybir.AluOpType.add
+MIN = mybir.AluOpType.min
 IS_GE = mybir.AluOpType.is_ge
 EXP = mybir.ActivationFunctionType.Exp
 COPY = mybir.ActivationFunctionType.Copy
-X = mybir.AxisListType.X
 
 P = 128
 HEADS = 2
@@ -24,6 +23,7 @@ BLOCKS = TOKENS // P
 PER = PIECE // P
 VROW = 144
 SLACK = 1.02
+TO_SHIFT = -SLACK / (2.0 * math.sqrt(P))
 STEP = 4
 AHEAD = 2
 LAG = PER + 2 * PER
@@ -58,10 +58,8 @@ def tile_pagedattention_b_kernel(tc, kv, scale, q, offs, out):
         nc.gpsimd.affine_select(
             out=causal[:], in_=causal[:], pattern=[[1, P]], compare_op=IS_GE, fill=0.0, base=0, channel_multiplier=-1
         )
-        half = held.tile([P, PIECES], F32, name="half")
-        nc.gpsimd.memset(half[:], 0.5)
         warm = held.tile([P, 1], F32, name="warm")
-        nc.scalar.activation(warm[:], half[:, 0:1], EXP)
+        nc.scalar.activation(warm[:], ones[:, 0:1], EXP)
 
         def load_window(row, name):
             window = held.tile([P, SLOTS], F32, name="window_" + name)
@@ -87,14 +85,13 @@ def tile_pagedattention_b_kernel(tc, kv, scale, q, offs, out):
             for p in range(1, PIECES):
                 v_factors[h].append(load_factors((HEADS + h) * P, "v%d" % h, p))
 
-        keys, values_t, shift, q_norm, q_factor, k_norm = [], [], [], [], [], []
+        keys, values_t, shift, q_part, k_part = [], [], [], [], []
         for h in range(HEADS):
             keys.append(held.tile([P, TOKENS], BF16, name="keys%d" % h))
             values_t.append(held.tile([P, BLOCKS, VROW], BF16, name="values_t%d" % h))
             shift.append(held.tile([P, PIECES], F32, name="shift%d" % h))
-            q_norm.append(held.tile([P, PIECES], F32, name="q_norm%d" % h))
-            q_factor.append(held.tile([P, PIECES], F32, name="q_factor%d" % h))
-            k_norm.append(held.tile([P, PIECES], F32, name="k_norm%d" % h))
+            q_part.append(held.tile([P, PIECES], F32, name="q_part%d" % h))
+            k_part.append(held.tile([P, PIECES], F32, name="k_part%d" % h))
             nc.gpsimd.memset(values_t[h][:, :, P : P + 1], 1.0)
 
         def dequantise(window, factors, p, rounded):
@@ -111,9 +108,9 @@ def tile_pagedattention_b_kernel(tc, kv, scale, q, offs, out):
 
         passed = {}
 
-        def largest(norms, result):
+        def part_of_shift(norms, so_far, result):
             spent = work.tile([P, PIECE], BF16, name="spent")
-            nc.vector.tensor_scalar(spent[:], norms[:], 1.0, None, op0=MULT, op1=MAX, accum_out=result)
+            nc.vector.tensor_scalar(spent[:], norms[:], TO_SHIFT, so_far, op0=MULT, op1=MIN, accum_out=result)
 
         def query_norms(h, c):
             squares = prep.tile([P, PIECE], BF16, name="q_squares", tag="prep")
@@ -121,12 +118,7 @@ def tile_pagedattention_b_kernel(tc, kv, scale, q, offs, out):
             nc.vector.tensor_tensor(squares[:], columns, columns, MULT)
             norms = scores.tile([P, PIECE], BF16, name="q_norms", tag="st")
             nc.tensor.matmul(norms[:], lhsT=ones[:], rhs=squares[:], start=True, stop=True)
-            largest(norms, q_norm[h][:, c : c + 1])
-
-        def query_factors(h):
-            q_root = small.tile([P, PIECES], F32, name="q_root")
-            nc.gpsimd.tensor_tensor(q_root[:], q_norm[h][:], half[:], POW)
-            nc.gpsimd.tensor_scalar(q_factor[h][:], q_root[:], -math.sqrt(SLACK / P), None, op0=MULT)
+            part_of_shift(norms, None, q_part[h][:, c : c + 1])
 
         def keys_gather(h, p):
             piece = keys[h][:, p * PIECE : (p + 1) * PIECE]
@@ -141,15 +133,9 @@ def tile_pagedattention_b_kernel(tc, kv, scale, q, offs, out):
             passed[("norms", h, p)] = norms
 
         def keys_shift(h, p):
-            largest(passed[("norms", h, p)], k_norm[h][:, p : p + 1])
-            seen = k_norm[h][:, 0:1]
-            if p > 0:
-                seen_so_far = small.tile([P, 1], F32, name="seen_so_far")
-                nc.vector.reduce_max(seen_so_far[:], k_norm[h][:, 0 : p + 1], axis=X)
-                seen = seen_so_far[:]
-            k_root = small.tile([P, 1], F32, name="k_root")
-            nc.gpsimd.tensor_tensor(k_root[:], seen, half[:, 0:1], POW)
-            nc.gpsimd.tensor_tensor(shift[h][:, p : p + 1], k_root[:], q_factor[h][:, p : p + 1], MULT)
+            so_far = k_part[h][:, p - 1 : p] if p > 0 else None
+            part_of_shift(passed[("norms", h, p)], so_far, k_part[h][:, p : p + 1])
+            nc.vector.tensor_tensor(shift[h][:, p : p + 1], k_part[h][:, p : p + 1], q_part[h][:, p : p + 1], ADD)
 
         def values_gather(h, p):
             passed[("values", h, p)] = dequantise(v_window[h], v_factors[h][p], p, None)
@@ -254,7 +240,6 @@ def tile_pagedattention_b_kernel(tc, kv, scale, q, offs, out):
         for h in range(HEADS):
             for c in range(PIECES):
                 query_norms(h, c)
-            query_factors(h)
         preparations = []
         for h in range(HEADS):
             for stages, p in ((KEYS_STAGES, 0), (KEYS_STAGES, 1), (KEYS_STAGES, 2), (VALUES_STAGES, 0), (KEYS_STAGES, 3)):

@@ -51,15 +51,15 @@ def tile_pagedattention_b_kernel(tc, kv, scale, q, offs, out):
         make_identity(nc, ident_bf[:])
         ident_f = held.tile([P, P], F32, name="ident_f")
         make_identity(nc, ident_f[:])
-        ones = held.tile([P, P], BF16, name="ones")
-        nc.gpsimd.memset(ones[:], 1.0)
+        weigher = held.tile([P, P], BF16, name="weigher")
+        nc.gpsimd.memset(weigher[:], TO_SHIFT)
         causal = held.tile([P, P], BF16, name="causal")
         nc.gpsimd.memset(causal[:], 1.0)
         nc.gpsimd.affine_select(
             out=causal[:], in_=causal[:], pattern=[[1, P]], compare_op=IS_GE, fill=0.0, base=0, channel_multiplier=-1
         )
         warm = held.tile([P, 1], F32, name="warm")
-        nc.scalar.activation(warm[:], ones[:, 0:1], EXP)
+        nc.scalar.activation(warm[:], weigher[:, 0:1], EXP)
 
         def load_window(row, name):
             window = held.tile([P, SLOTS], F32, name="window_" + name)
@@ -85,13 +85,12 @@ def tile_pagedattention_b_kernel(tc, kv, scale, q, offs, out):
             for p in range(1, PIECES):
                 v_factors[h].append(load_factors((HEADS + h) * P, "v%d" % h, p))
 
-        keys, values_t, shift, q_part, k_part = [], [], [], [], []
+        keys, values_t, shift, q_part = [], [], [], []
         for h in range(HEADS):
             keys.append(held.tile([P, TOKENS], BF16, name="keys%d" % h))
             values_t.append(held.tile([P, BLOCKS, VROW], BF16, name="values_t%d" % h))
             shift.append(held.tile([P, PIECES], F32, name="shift%d" % h))
             q_part.append(held.tile([P, PIECES], F32, name="q_part%d" % h))
-            k_part.append(held.tile([P, PIECES], F32, name="k_part%d" % h))
             nc.gpsimd.memset(values_t[h][:, :, P : P + 1], 1.0)
 
         def dequantise(window, factors, p, rounded):
@@ -108,17 +107,17 @@ def tile_pagedattention_b_kernel(tc, kv, scale, q, offs, out):
 
         passed = {}
 
-        def part_of_shift(norms, so_far, result):
+        def lowest(weighed, added, so_far, result):
             spent = work.tile([P, PIECE], BF16, name="spent")
-            nc.vector.tensor_scalar(spent[:], norms[:], TO_SHIFT, so_far, op0=MULT, op1=MIN, accum_out=result)
+            nc.vector.tensor_scalar(spent[:], weighed[:], added, so_far, op0=ADD, op1=MIN, accum_out=result)
 
         def query_norms(h, c):
             squares = prep.tile([P, PIECE], BF16, name="q_squares", tag="prep")
             columns = queries[h][:, c * PIECE : (c + 1) * PIECE]
             nc.vector.tensor_tensor(squares[:], columns, columns, MULT)
             norms = scores.tile([P, PIECE], BF16, name="q_norms", tag="st")
-            nc.tensor.matmul(norms[:], lhsT=ones[:], rhs=squares[:], start=True, stop=True)
-            part_of_shift(norms, None, q_part[h][:, c : c + 1])
+            nc.tensor.matmul(norms[:], lhsT=weigher[:], rhs=squares[:], start=True, stop=True)
+            lowest(norms, 0.0, q_part[h][:, c - 1 : c] if c > 0 else None, q_part[h][:, c : c + 1])
 
         def keys_gather(h, p):
             piece = keys[h][:, p * PIECE : (p + 1) * PIECE]
@@ -129,13 +128,12 @@ def tile_pagedattention_b_kernel(tc, kv, scale, q, offs, out):
 
         def keys_column_sums(h, p):
             norms = scores.tile([P, PIECE], BF16, name="norms", tag="st")
-            nc.tensor.matmul(norms[:], lhsT=ones[:], rhs=passed[("squares", h, p)][:], start=True, stop=True)
+            nc.tensor.matmul(norms[:], lhsT=weigher[:], rhs=passed[("squares", h, p)][:], start=True, stop=True)
             passed[("norms", h, p)] = norms
 
         def keys_shift(h, p):
-            so_far = k_part[h][:, p - 1 : p] if p > 0 else None
-            part_of_shift(passed[("norms", h, p)], so_far, k_part[h][:, p : p + 1])
-            nc.vector.tensor_tensor(shift[h][:, p : p + 1], k_part[h][:, p : p + 1], q_part[h][:, p : p + 1], ADD)
+            of_queries = q_part[h][:, PIECES - 1 : PIECES]
+            lowest(passed[("norms", h, p)], of_queries, shift[h][:, p - 1 : p] if p > 0 else None, shift[h][:, p : p + 1])
 
         def values_gather(h, p):
             passed[("values", h, p)] = dequantise(v_window[h], v_factors[h][p], p, None)

@@ -78,10 +78,11 @@ def tile_pagedattention_b_kernel(tc, kv, scale, q, offs, out):
         for h in range(HEADS):
             k_factors.append([load_factors(h * P, "k%d" % h, 0)])
             k_window.append(load_window(h * P, "k%d" % h))
-            for p in range(1, PIECES):
+            for p in range(1, PIECES - 1):
                 k_factors[h].append(load_factors(h * P, "k%d" % h, p))
             v_factors.append([load_factors((HEADS + h) * P, "v%d" % h, 0)])
             v_window.append(load_window((HEADS + h) * P, "v%d" % h))
+            k_factors[h].append(load_factors(h * P, "k%d" % h, PIECES - 1))
             for p in range(1, PIECES):
                 v_factors[h].append(load_factors((HEADS + h) * P, "v%d" % h, p))
 

import math

import concourse.mybir as mybir
from concourse.masks import make_identity

F32 = mybir.dt.float32
BF16 = mybir.dt.bfloat16
U16 = mybir.dt.uint16
MULT = mybir.AluOpType.mult
ADD = mybir.AluOpType.add
MIN = mybir.AluOpType.min
IS_GE = mybir.AluOpType.is_ge
EXP = mybir.ActivationFunctionType.Exp
COPY = mybir.ActivationFunctionType.Copy

P = 128
HEADS = 2
SLOTS = 4096
TOKENS = 2048
PIECE = 512
PIECES = TOKENS // PIECE
BLOCKS = TOKENS // P
PER = PIECE // P
VROW = 144
SLACK = 1.02
TO_SHIFT = -SLACK / (2.0 * math.sqrt(P))
STEP = 4
AHEAD = 2
LAG = PER + 2 * PER

FLOPS = HEADS * 2 * 2 * P * (TOKENS * (TOKENS + 1) // 2)
BYTES = 2 * HEADS * P * TOKENS * (4 + 4) + HEADS * P * TOKENS * (2 + 4) + TOKENS * 2


def tile_pagedattention_b_kernel(tc, kv, scale, q, offs, out):
    nc = tc.nc
    with (
        tc.tile_pool(name="held", bufs=1) as held,
        tc.tile_pool(name="work", bufs=4) as work,
        tc.tile_pool(name="prep", bufs=3) as prep,
        tc.tile_pool(name="small", bufs=4) as small,
        tc.tile_pool(name="weights", bufs=LAG + 4) as weights,
        tc.tile_pool(name="stairs", bufs=3) as stairs_pool,
        tc.psum_pool(name="scores", bufs=5) as scores,
        tc.psum_pool(name="sums", bufs=3) as sums,
    ):
        offsets = held.tile([P, TOKENS // 16], U16, name="offsets")
        nc.sync.dma_start(offsets[:], offs)

        ident_bf = held.tile([P, P], BF16, name="ident_bf")
        make_identity(nc, ident_bf[:])
        ident_f = held.tile([P, P], F32, name="ident_f")
        make_identity(nc, ident_f[:])
        weigher = held.tile([P, P], BF16, name="weigher")
        nc.gpsimd.memset(weigher[:], TO_SHIFT)
        causal = held.tile([P, P], BF16, name="causal")
        nc.gpsimd.memset(causal[:], 1.0)
        nc.gpsimd.affine_select(
            out=causal[:], in_=causal[:], pattern=[[1, P]], compare_op=IS_GE, fill=0.0, base=0, channel_multiplier=-1
        )
        warm = held.tile([P, 1], F32, name="warm")
        nc.scalar.activation(warm[:], weigher[:, 0:1], EXP)

        def load_window(row, name):
            window = held.tile([P, SLOTS], F32, name="window_" + name)
            nc.sync.dma_start(window[:], kv[row : row + P, :])
            return window

        def load_factors(row, name, p):
            factors = held.tile([P, PIECE], F32, name="factors_%s%d" % (name, p))
            nc.sync.dma_start(factors[:], scale[row : row + P, p * PIECE : (p + 1) * PIECE])
            return factors

        queries, k_window, v_window, k_factors, v_factors = [], [], [], [], []
        for h in range(HEADS):
            queries.append(held.tile([P, TOKENS], BF16, name="queries%d" % h))
            nc.sync.dma_start(queries[h][:], q[h * P : (h + 1) * P, :])
        for h in range(HEADS):
            k_factors.append([load_factors(h * P, "k%d" % h, 0)])
            k_window.append(load_window(h * P, "k%d" % h))
            for p in range(1, PIECES - 1):
                k_factors[h].append(load_factors(h * P, "k%d" % h, p))
            v_factors.append([load_factors((HEADS + h) * P, "v%d" % h, 0)])
            v_window.append(load_window((HEADS + h) * P, "v%d" % h))
            k_factors[h].append(load_factors(h * P, "k%d" % h, PIECES - 1))
            for p in range(1, PIECES):
                v_factors[h].append(load_factors((HEADS + h) * P, "v%d" % h, p))

        keys, values_t, shift, q_part = [], [], [], []
        for h in range(HEADS):
            keys.append(held.tile([P, TOKENS], BF16, name="keys%d" % h))
            values_t.append(held.tile([P, BLOCKS, VROW], BF16, name="values_t%d" % h))
            shift.append(held.tile([P, PIECES], F32, name="shift%d" % h))
            q_part.append(held.tile([P, PIECES], F32, name="q_part%d" % h))
            nc.gpsimd.memset(values_t[h][:, :, P : P + 1], 1.0)

        def dequantise(window, factors, p, rounded):
            wide = PIECE // 16
            product = prep.tile([P, PIECE], F32, name="product", tag="prep")
            nc.vector.tensor_tensor(
                product[:], window[:].indirect(offsets[:, p * wide : (p + 1) * wide]), factors[:], MULT
            )
            if rounded is None:
                values = prep.tile([P, PIECE], BF16, name="values", tag="prep")
                rounded = values[:]
            nc.vector.tensor_copy(rounded, product[:])
            return rounded

        passed = {}

        def lowest(weighed, added, so_far, result):
            spent = work.tile([P, PIECE], BF16, name="spent")
            nc.vector.tensor_scalar(spent[:], weighed[:], added, so_far, op0=ADD, op1=MIN, accum_out=result)

        def query_norms(h, c):
            squares = prep.tile([P, PIECE], BF16, name="q_squares", tag="prep")
            columns = queries[h][:, c * PIECE : (c + 1) * PIECE]
            nc.vector.tensor_tensor(squares[:], columns, columns, MULT)
            norms = scores.tile([P, PIECE], BF16, name="q_norms", tag="st")
            nc.tensor.matmul(norms[:], lhsT=weigher[:], rhs=squares[:], start=True, stop=True)
            lowest(norms, 0.0, q_part[h][:, c - 1 : c] if c > 0 else None, q_part[h][:, c : c + 1])

        def keys_gather(h, p):
            piece = keys[h][:, p * PIECE : (p + 1) * PIECE]
            dequantise(k_window[h], k_factors[h][p], p, piece)
            squares = prep.tile([P, PIECE], BF16, name="squares", tag="prep")
            nc.vector.tensor_tensor(squares[:], piece, piece, MULT)
            passed[("squares", h, p)] = squares

        def keys_column_sums(h, p):
            norms = scores.tile([P, PIECE], BF16, name="norms", tag="st")
            nc.tensor.matmul(norms[:], lhsT=weigher[:], rhs=passed[("squares", h, p)][:], start=True, stop=True)
            passed[("norms", h, p)] = norms

        def keys_shift(h, p):
            of_queries = q_part[h][:, PIECES - 1 : PIECES]
            lowest(passed[("norms", h, p)], of_queries, shift[h][:, p - 1 : p] if p > 0 else None, shift[h][:, p : p + 1])

        def values_gather(h, p):
            passed[("values", h, p)] = dequantise(v_window[h], v_factors[h][p], p, None)

        def values_flip(h, p):
            flipped = scores.tile([P, PER, P], BF16, name="flipped", tag="st")
            for k in range(PER):
                nc.tensor.transpose(flipped[:, k, :], passed[("values", h, p)][:, k * P : (k + 1) * P], ident_bf[:])
            passed[("flipped", h, p)] = flipped

        def values_keep(h, p):
            nc.vector.tensor_copy(values_t[h][:, p * PER : (p + 1) * PER, 0:P], passed[("flipped", h, p)][:])

        KEYS_STAGES = ((0, keys_gather), (6, keys_column_sums), (7, keys_shift))
        VALUES_STAGES = ((0, values_gather), (6, values_flip), (7, values_keep))

        chunks = [(h, c) for h in range(HEADS) for c in range(PIECES)]
        tiles = [(x, jb) for x in range(len(chunks)) for jb in range(PER * (chunks[x][1] + 1))]
        made = {}
        sums_of = {}
        agenda = {}

        def write_at(step, call, *args):
            agenda.setdefault(step, []).append((call, args))

        def scores_and_weights(x, jb):
            h, c = chunks[x]
            first = max(jb - PER * c, 0)
            lo = first * P
            st = scores.tile([P, PIECE], F32, name="st")
            nc.tensor.matmul(
                st[:, lo:],
                lhsT=keys[h][:, jb * P : (jb + 1) * P],
                rhs=queries[h][:, c * PIECE + lo : (c + 1) * PIECE],
                start=True,
                stop=True,
            )
            if jb < PER * c:
                whole = weights.tile([P, PIECE], BF16, name="e")
                e = whole[:]
            else:
                if first == 0:
                    passed[("stairs", x)] = stairs_pool.tile([P, PER, PIECE], BF16, name="stairs")
                e = passed[("stairs", x)][:, first, 0 : PIECE - lo]
            nc.scalar.activation(e, st[:, lo:], EXP, bias=shift[h][:, c : c + 1], scale=1.0 / math.sqrt(P))
            if first == PER - 1:
                on_diagonal = passed[("stairs", x)][:, :, 0:P]
                nc.vector.tensor_tensor(on_diagonal, on_diagonal, causal[:].unsqueeze(1).to_broadcast([P, PER, P]), MULT)
            made[(x, jb)] = e

        def normalise(x, a):
            h, c = chunks[x]
            out_t, normal, inverse = sums_of[x]
            normal[a] = work.tile([P, 2, P], F32, name="normal")
            if h == 0:
                for b in range(2):
                    nc.scalar.activation(normal[a][:, b, :], out_t[a][:, b, 0:P], COPY, scale=inverse[a][:, b, :])
            else:
                nc.vector.tensor_tensor(normal[a][:], out_t[a][:, :, 0:P], inverse[a][:].to_broadcast([P, 2, P]), MULT)

        def turn(x, a):
            normal = sums_of[x][1]
            turned = scores.tile([P, 2 * P], F32, name="turned", tag="st")
            for b in range(2):
                nc.tensor.transpose(turned[:, b * P : (b + 1) * P], normal[a][:, b, :], ident_f[:])
            passed[("turned", x, a)] = turned

        def store(x, a):
            h, c = chunks[x]
            staged = work.tile([P, 2 * P], F32, name="staged")
            if h == 0:
                nc.scalar.copy(staged[:], passed[("turned", x, a)][:])
            else:
                nc.vector.tensor_copy(staged[:], passed[("turned", x, a)][:])
            lo = c * PIECE + a * 2 * P
            nc.sync.dma_start(out[h * P : (h + 1) * P, lo : lo + 2 * P], staged[:])

        def weighted_sums(x, jb, step):
            h, c = chunks[x]
            first = max(jb - PER * c, 0)
            e = made[(x, jb)]
            if jb == 0:
                out_t = [sums.tile([P, 2, P + 1], F32, name="out_t%d" % a, tag="out_t") for a in range(PER // 2)]
                sums_of[x] = (out_t, [None, None], [None, None])
            out_t, normal, inverse = sums_of[x]
            for r in range(first, PER):
                nc.tensor.matmul(
                    out_t[r // 2][:, r % 2, :],
                    lhsT=e[:, (r - first) * P : (r - first + 1) * P],
                    rhs=values_t[h][:, jb, 0 : P + 1],
                    start=(jb == 0 and r % 2 == 0),
                    stop=(jb == PER * c + r and r % 2 == 1),
                )
            if jb >= PER * c and first % 2 == 1:
                a = first // 2
                inverse[a] = small.tile([P, 2, 1], F32, name="inverse")
                nc.vector.reciprocal(inverse[a][:], out_t[a][:, :, P : P + 1])
                write_at(step + 1, normalise, x, a)
                write_at(step + 3, turn, x, a)
                write_at(step + 4, store, x, a)

        for h in range(HEADS):
            for c in range(PIECES):
                query_norms(h, c)
        preparations = []
        for h in range(HEADS):
            for stages, p in ((KEYS_STAGES, 0), (KEYS_STAGES, 1), (KEYS_STAGES, 2), (VALUES_STAGES, 0), (KEYS_STAGES, 3)):
                preparations.append((stages, h, p))
            preparations.extend([(VALUES_STAGES, h, p) for p in range(1, PIECES)])
        for k in range(len(preparations)):
            stages, h, p = preparations[k]
            for wait, call in stages:
                write_at((k - AHEAD) * STEP + wait, call, h, p)
        LAST = 4
        for n in range(-AHEAD * STEP, len(tiles) + LAG + LAST):
            if 0 <= n < len(tiles):
                scores_and_weights(*tiles[n])
            if LAG <= n < len(tiles) + LAG:
                weighted_sums(*tiles[n - LAG], n)
            for call, args in agenda.get(n, []):
                call(*args)
